import numpy as np
import ml_dtypes


def mxq(x, axis, fmt="e4m3"):
    dtype, down = {"e4m3": (ml_dtypes.float8_e4m3fn, 7), "e5m2": (ml_dtypes.float8_e5m2, 14)}[fmt]
    v = np.moveaxis(np.asarray(x, np.float32).astype(ml_dtypes.bfloat16).astype(np.float64), axis, -1)
    blocks = v.reshape(v.shape[:-1] + (-1, 32))
    amax = np.abs(blocks).max(-1, keepdims=True)
    byte = np.maximum(np.where(amax > 0, np.frexp(amax)[1] - 1 + 127, 0) - down, 1)
    scale = np.exp2(byte - 127.0)
    codes = (blocks / scale).astype(np.float32).astype(dtype).astype(np.float64)
    return np.moveaxis((codes * scale).reshape(v.shape), -1, axis)


WIDE = False


def mx_kscale(k):
    if not WIDE:
        return np.ones(k)
    levels = np.array([10, -10, 5, -5, 0])
    if k % 512:
        return np.exp2(np.random.permutation(np.resize(levels, k // 32))).repeat(32)
    a = np.empty((k // 512, 16))
    for p in range(k // 512):
        a[p, :8] = np.random.permutation(np.resize(levels, 8))
        for g in range(8):
            far = levels[np.abs(levels - a[p, g]) >= 10]
            a[p, g + 8] = far[np.random.randint(len(far))]
    return np.exp2(a.ravel()).repeat(32)


BF16 = ml_dtypes.bfloat16


def bf(x):
    return np.asarray(x, np.float32).astype(BF16)


def f64(x):
    return np.asarray(x).astype(np.float64)


B, C, K, L, R = 4, 64, 512, 16, 128


def transition():
    g = np.exp(2.5 * np.random.standard_normal((K, K)))
    return g / g.sum(1, keepdims=True)


def setup_inputs():
    s = mx_kscale(K)
    x = np.random.standard_normal((B, C, K, L)) * 2.0 * s[None, None, :, None]
    return {'x': bf(x.reshape(B, C, K * L)),
            'support0': bf(transition() * s[:, None] / s[None, :]),
            'support1': bf(transition() * s[:, None] / s[None, :])}


def two_hops(xq, a):
    aq = mxq(f64(a).T, 0, 'e4m3')
    x1 = xq @ aq
    x2 = mxq(x1, 2, 'e4m3') @ aq
    return x1, x2


def reference(x, support0, support1):
    xr = f64(x).reshape(B, C, K, L).transpose(0, 3, 1, 2).reshape(B * L, C, K)
    xq = mxq(xr, 2, 'e4m3')
    f1, f2 = two_hops(xq, support0)
    g1, g2 = two_hops(xq, support1)
    return f1, f2, g1, g2

@@ -1,0 +1,251 @@
+from contextlib import ExitStack
+
+import concourse.mybir as mybir
+from concourse.masks import make_identity
+
+BF16 = mybir.dt.bfloat16
+F32 = mybir.dt.float32
+U32 = mybir.dt.uint32
+U8 = mybir.dt.uint8
+FP8X4 = mybir.dt.float8_e4m3fn_x4
+
+P = 128
+PACK = 4
+BATCHES, CHANNELS, NODES, STEPS = 4, 64, 512, 16
+assert NODES == P * PACK
+PAIR = P // CHANNELS
+
+ROWS = 4
+PANEL = P * ROWS
+PANEL_STEPS = PANEL // CHANNELS
+HALVES = STEPS // PANEL_STEPS
+PAIRS = BATCHES // PAIR
+GROUPS = PAIRS * HALVES
+X_BANKS = PANEL_STEPS // 2
+WORD_STEPS = STEPS // 2
+LAG = 4
+
+FLOPS = 4 * 2 * BATCHES * STEPS * CHANNELS * NODES * NODES
+
+
+def tile_adaptivegcn_pb_t_kernel(
+    tc, x, support0, support1, out_0, out_1, out_2, out_3
+):
+    nc = tc.nc
+    supports = (support0, support1)
+    hop1_outs = (out_0, out_2)
+    hop2_outs = (out_1, out_3)
+
+    with ExitStack() as ctx:
+        ctx.enter_context(tc.manual_schedule())
+        resident = ctx.enter_context(tc.tile_pool(name="resident", bufs=1))
+        x_pool = ctx.enter_context(tc.tile_pool(name="x_pool", bufs=2))
+        hop1_pool = ctx.enter_context(tc.tile_pool(name="hop1_pool", bufs=LAG + 2))
+        store_pool = ctx.enter_context(tc.tile_pool(name="store_pool", bufs=6))
+        psum_quant = ctx.enter_context(tc.psum_pool(name="psum_quant", bufs=4))
+        psum_store = ctx.enter_context(tc.psum_pool(name="psum_store", bufs=4))
+
+        def load_support(s):
+            rows = resident.tile([P, PACK, NODES], BF16, name="support_rows_%d" % s)
+            nc.sync.dma_start(out=rows[:], in_=supports[s].rearrange("(p t) v -> p t v", t=PACK))
+            return rows
+
+        def load_x(pair):
+            rows = x.rearrange("b c f -> (b c) f")[pair * P : (pair + 1) * P]
+            tile = resident.tile([P, NODES * STEPS], BF16, name="x_rows_%d" % pair)
+            for u in range(2):
+                cols = slice(u * NODES * STEPS // 2, (u + 1) * NODES * STEPS // 2)
+                nc.sync.dma_start(out=tile[:, cols], in_=rows[:, cols])
+            return tile
+
+        support_rows = {0: load_support(0)}
+        x_rows = {0: load_x(0)}
+        support_rows[1] = load_support(1)
+        x_rows[1] = load_x(1)
+
+        ident_f32 = resident.tile([P, P], F32)
+        make_identity(nc, ident_f32[:])
+        sort_channels = resident.tile([P, P], F32)
+        nc.vector.tensor_copy(
+            out=sort_channels[:].rearrange("q (b j c) -> q b j c", j=ROWS, b=PAIR),
+            in_=ident_f32[:].rearrange("q (b c j) -> q b j c", j=ROWS, b=PAIR),
+        )
+
+        support_codes = {}
+        support_scales = {}
+
+        def quantise_support(s):
+            grouped = resident.tile(
+                [P, NODES, PACK], BF16, name="support_grouped_%d" % s, align_bytes=64
+            )
+            words = grouped[:].rearrange("p w k -> p (w k)").bitcast(F32)
+            for half in range(2):
+                flipped = psum_store.tile([P, 2, 2, P], F32, tag="store_bank")
+                for i in range(2):
+                    row = support_rows[s][:, 2 * half + i, :].bitcast(F32)
+                    for u in range(2):
+                        nc.tensor.transpose(flipped[:, i, u, :], row[:, u::2], ident_f32[:])
+                copy = nc.vector.tensor_copy if half == 0 else nc.scalar.copy
+                copy(
+                    out=words[:, half * NODES : (half + 1) * NODES].rearrange(
+                        "p (i m u) -> p i m u", i=2, u=2
+                    ),
+                    in_=flipped[:].rearrange("p i u m -> p i m u"),
+                )
+            support_codes[s] = resident.tile(
+                [P, NODES], U32, name="support_codes_%d" % s, align_bytes=64
+            )
+            support_scales[s] = resident.tile(
+                [P, NODES], U8, name="support_scales_%d" % s, align_bytes=64
+            )
+            nc.vector.quantize_mx(
+                out=support_codes[s][:].bitcast(FP8X4),
+                scales=support_scales[s][:],
+                in_=grouped[:].rearrange("p w t -> p (w t)"),
+            )
+
+        x_grouped = {}
+        x_codes = {}
+        x_scales = {}
+
+        def new_group(group):
+            x_grouped[group] = x_pool.tile(
+                [P, PAIR, PANEL * PACK], BF16, name="x_grouped", align_bytes=64
+            )
+            x_codes[group] = x_pool.tile([P, PAIR, PANEL], U32, name="x_codes", align_bytes=64)
+            x_scales[group] = x_pool.tile([P, PAIR, PANEL], U8, name="x_scales", align_bytes=64)
+
+        def flip_x(group, i):
+            pair, half = divmod(group, HALVES)
+            bank = psum_quant.tile([P, PACK, P], F32, name="x_flipped", tag="quant_bank")
+            words = x_rows[pair][:].bitcast(F32).rearrange("r (k w) -> r k w", w=WORD_STEPS)
+            for t in range(PACK):
+                nc.tensor.transpose(
+                    bank[:, t, :], words[:, t::PACK, half * X_BANKS + i], sort_channels[:]
+                )
+            return bank
+
+        def sort_x(copy, group, i, bank):
+            halves = bank[:].bitcast(BF16).rearrange("p t (bj c e) -> p e bj c t", e=2, c=P // (PAIR * ROWS))
+            sorted_steps = x_grouped[group][:].rearrange(
+                "p b (j i e c t) -> p i e (b j) c t", j=ROWS, i=X_BANKS, e=2, t=PACK
+            )
+            for e in range(2):
+                copy(out=sorted_steps[:, i, e], in_=halves[:, e])
+
+        def quantise_x(group, b):
+            nc.vector.quantize_mx(
+                out=x_codes[group][:, b, :].bitcast(FP8X4),
+                scales=x_scales[group][:, b, :],
+                in_=x_grouped[group][:, b, :],
+            )
+
+        def product_to_hbm(codes, scales, s, j, staged, out, group, b, alone):
+            bank = psum_store.tile([P, NODES], F32, tag="store_bank")
+            nc.tensor.matmul_mx(
+                out=bank[:],
+                lhsT=codes.bitcast(FP8X4),
+                lhsT_scale=scales,
+                rhs=support_codes[s][:].bitcast(FP8X4),
+                rhs_scale=support_scales[s][:],
+                start=True,
+                stop=True,
+            )
+            nc.scalar.copy(
+                out=staged[:, j, :].rearrange("p (m t) -> p m t", t=PACK),
+                in_=bank[:].rearrange("p (t m) -> p m t", t=PACK),
+            )
+            pair, half = divmod(group, HALVES)
+            first = (pair * PAIR + b) * STEPS + half * PANEL_STEPS
+            in_hbm = out[first : first + PANEL_STEPS].rearrange("l (c j) w -> (l c) j w", j=ROWS)
+            if alone:
+                nc.sync.dma_start(out=in_hbm[:, j, :], in_=staged[:, j, :])
+            elif j == ROWS - 1:
+                nc.sync.dma_start(out=in_hbm, in_=staged[:])
+
+        def flipped_first_hop(group, s, b, j):
+            cols = slice(j * P, (j + 1) * P)
+            bank = psum_quant.tile([P, PACK, P], F32, name="hop1_flipped", tag="quant_bank")
+            for t in range(PACK):
+                nodes = slice(t * P, (t + 1) * P)
+                nc.tensor.matmul_mx(
+                    out=bank[:, t, :],
+                    lhsT=support_codes[s][:, nodes].bitcast(FP8X4),
+                    lhsT_scale=support_scales[s][:, nodes],
+                    rhs=x_codes[group][:, b, cols].bitcast(FP8X4),
+                    rhs_scale=x_scales[group][:, b, cols],
+                    start=True,
+                    stop=True,
+                )
+            grouped = hop1_pool.tile([P, P, PACK], BF16, name="hop1_grouped", align_bytes=64)
+            nc.vector.tensor_copy(out=grouped[:], in_=bank[:].rearrange("p t r -> p r t"))
+            return grouped
+
+        def quantise_hop1(grouped):
+            codes = hop1_pool.tile([P, P], U32, name="hop1_codes", align_bytes=64)
+            scales = hop1_pool.tile([P, P], U8, name="hop1_scales", align_bytes=64)
+            nc.vector.quantize_mx(
+                out=codes[:].bitcast(FP8X4),
+                scales=scales[:],
+                in_=grouped[:].rearrange("p r t -> p (r t)"),
+            )
+            return codes, scales
+
+        quantise_support(0)
+        new_group(0)
+        for i in range(X_BANKS):
+            copy = nc.scalar.copy if i % 2 else nc.vector.tensor_copy
+            sort_x(copy, 0, i, flip_x(0, i))
+        for b in range(PAIR):
+            quantise_x(0, b)
+
+        jobs = [(group, s, b) for group in range(GROUPS) for s in range(2) for b in range(PAIR)]
+        assert len(jobs) == GROUPS * X_BANKS
+        quarters = len(jobs) * ROWS
+        staging = {}
+        hop1_grouped = {}
+        hop1_quantised = {}
+        for n in range(quarters + LAG):
+            alone = n >= quarters - ROWS
+            if n < quarters:
+                job, j = divmod(n, ROWS)
+                group, s, b = jobs[job]
+                cols = slice(j * P, (j + 1) * P)
+                if j == 0:
+                    staging[1, job] = store_pool.tile([P, ROWS, NODES], F32, name="staged")
+                product_to_hbm(
+                    x_codes[group][:, b, cols],
+                    x_scales[group][:, b, cols],
+                    s,
+                    j,
+                    staging[1, job],
+                    hop1_outs[s],
+                    group,
+                    b,
+                    alone,
+                )
+            if n >= LAG:
+                job, j = divmod(n - LAG, ROWS)
+                group, s, b = jobs[job]
+                codes, scales = hop1_quantised[n - LAG]
+                if j == 0:
+                    staging[2, job] = store_pool.tile([P, ROWS, NODES], F32, name="staged")
+                product_to_hbm(
+                    codes[:], scales[:], s, j, staging[2, job], hop2_outs[s], group, b, alone
+                )
+            if n < quarters:
+                job, j = divmod(n, ROWS)
+                group, s, b = jobs[job]
+                hop1_grouped[n] = flipped_first_hop(group, s, b, j)
+            if 1 <= n <= quarters:
+                hop1_quantised[n - 1] = quantise_hop1(hop1_grouped[n - 1])
+            if n < quarters:
+                i = job % X_BANKS
+                if group + 1 < GROUPS and j == 0:
+                    if i == 0:
+                        new_group(group + 1)
+                    sort_x(nc.vector.tensor_copy, group + 1, i, flip_x(group + 1, i))
+                if group + 1 < GROUPS and i == X_BANKS - 1 and 1 <= j <= PAIR:
+                    quantise_x(group + 1, j - 1)
+                if n == ROWS - 1:
+                    quantise_support(1)

@@ -23,7 +23,7 @@ PAIRS = BATCHES // PAIR
 GROUPS = PAIRS * HALVES
 X_BANKS = PANEL_STEPS // 2
 WORD_STEPS = STEPS // 2
-LAG = 4
+LAG = 2
 
 FLOPS = 4 * 2 * BATCHES * STEPS * CHANNELS * NODES * NODES
 
@@ -40,10 +40,11 @@ def tile_adaptivegcn_pb_t_kernel(
         ctx.enter_context(tc.manual_schedule())
         resident = ctx.enter_context(tc.tile_pool(name="resident", bufs=1))
         x_pool = ctx.enter_context(tc.tile_pool(name="x_pool", bufs=2))
-        hop1_pool = ctx.enter_context(tc.tile_pool(name="hop1_pool", bufs=LAG + 2))
-        store_pool = ctx.enter_context(tc.tile_pool(name="store_pool", bufs=6))
-        psum_quant = ctx.enter_context(tc.psum_pool(name="psum_quant", bufs=4))
-        psum_store = ctx.enter_context(tc.psum_pool(name="psum_store", bufs=4))
+        hop1_pool = ctx.enter_context(tc.tile_pool(name="hop1_pool", bufs=LAG + 1))
+        rows_pool = ctx.enter_context(tc.tile_pool(name="rows_pool", bufs=2 * ROWS))
+        store_pool = ctx.enter_context(tc.tile_pool(name="store_pool", bufs=12))
+        psum_quant = ctx.enter_context(tc.psum_pool(name="psum_quant", bufs=3))
+        psum_store = ctx.enter_context(tc.psum_pool(name="psum_store", bufs=5))
 
         def load_support(s):
             rows = resident.tile([P, PACK, NODES], BF16, name="support_rows_%d" % s)
@@ -133,14 +134,14 @@ def tile_adaptivegcn_pb_t_kernel(
             for e in range(2):
                 copy(out=sorted_steps[:, i, e], in_=halves[:, e])
 
-        def quantise_x(group, b):
+        def quantise_x(group, b, cols=slice(0, PANEL)):
             nc.vector.quantize_mx(
-                out=x_codes[group][:, b, :].bitcast(FP8X4),
-                scales=x_scales[group][:, b, :],
-                in_=x_grouped[group][:, b, :],
+                out=x_codes[group][:, b, cols].bitcast(FP8X4),
+                scales=x_scales[group][:, b, cols],
+                in_=x_grouped[group][:, b, cols.start * PACK : cols.stop * PACK],
             )
 
-        def product_to_hbm(codes, scales, s, j, staged, out, group, b, alone):
+        def product_to_hbm(copy, codes, scales, s, j, staged, out, group, b, alone):
             bank = psum_store.tile([P, NODES], F32, tag="store_bank")
             nc.tensor.matmul_mx(
                 out=bank[:],
@@ -151,7 +152,7 @@ def tile_adaptivegcn_pb_t_kernel(
                 start=True,
                 stop=True,
             )
-            nc.scalar.copy(
+            copy(
                 out=staged[:, j, :].rearrange("p (m t) -> p m t", t=PACK),
                 in_=bank[:].rearrange("p (t m) -> p m t", t=PACK),
             )
@@ -163,31 +164,48 @@ def tile_adaptivegcn_pb_t_kernel(
             elif j == ROWS - 1:
                 nc.sync.dma_start(out=in_hbm, in_=staged[:])
 
-        def flipped_first_hop(group, s, b, j):
-            cols = slice(j * P, (j + 1) * P)
-            bank = psum_quant.tile([P, PACK, P], F32, name="hop1_flipped", tag="quant_bank")
-            for t in range(PACK):
-                nodes = slice(t * P, (t + 1) * P)
-                nc.tensor.matmul_mx(
-                    out=bank[:, t, :],
-                    lhsT=support_codes[s][:, nodes].bitcast(FP8X4),
-                    lhsT_scale=support_scales[s][:, nodes],
-                    rhs=x_codes[group][:, b, cols].bitcast(FP8X4),
-                    rhs_scale=x_scales[group][:, b, cols],
-                    start=True,
-                    stop=True,
+        def round_hop1(staged, j):
+            rows = rows_pool.tile([P, NODES], BF16, name="hop1_rows")
+            nc.gpsimd.tensor_scalar(
+                out=rows[:].rearrange("r (u m e) -> r u m e", u=2, e=2),
+                in0=staged[:, j, :].rearrange("r (m u e) -> r u m e", u=2, e=2),
+                scalar1=1.0,
+                scalar2=0.0,
+                op0=mybir.AluOpType.mult,
+                op1=mybir.AluOpType.add,
+            )
+            return rows
+
+        def flip_hop1(quarter_rows):
+            banks = []
+            for half in range(2):
+                bank = psum_quant.tile([P, 2, 2, P], F32, name="hop1_flipped", tag="quant_bank")
+                for i in range(2):
+                    words = quarter_rows[2 * half + i][:].bitcast(F32)
+                    for u in range(2):
+                        nc.tensor.transpose(
+                            bank[:, i, u, :], words[:, u * P : (u + 1) * P], ident_f32[:]
+                        )
+                banks.append(bank)
+            return banks
+
+        def group_hop1(banks):
+            grouped = hop1_pool.tile([P, PANEL * PACK], BF16, name="hop1_grouped", align_bytes=64)
+            words = grouped[:].bitcast(F32)
+            for half, bank in enumerate(banks):
+                nc.vector.tensor_copy(
+                    out=words[:, half * NODES : (half + 1) * NODES].rearrange(
+                        "p (i r u) -> p i r u", i=2, u=2
+                    ),
+                    in_=bank[:].rearrange("p i u r -> p i r u"),
                 )
-            grouped = hop1_pool.tile([P, P, PACK], BF16, name="hop1_grouped", align_bytes=64)
-            nc.vector.tensor_copy(out=grouped[:], in_=bank[:].rearrange("p t r -> p r t"))
             return grouped
 
         def quantise_hop1(grouped):
-            codes = hop1_pool.tile([P, P], U32, name="hop1_codes", align_bytes=64)
-            scales = hop1_pool.tile([P, P], U8, name="hop1_scales", align_bytes=64)
+            codes = hop1_pool.tile([P, PANEL], U32, name="hop1_codes", align_bytes=64)
+            scales = hop1_pool.tile([P, PANEL], U8, name="hop1_scales", align_bytes=64)
             nc.vector.quantize_mx(
-                out=codes[:].bitcast(FP8X4),
-                scales=scales[:],
-                in_=grouped[:].rearrange("p r t -> p (r t)"),
+                out=codes[:].bitcast(FP8X4), scales=scales[:], in_=grouped[:]
             )
             return codes, scales
 
@@ -196,56 +214,67 @@ def tile_adaptivegcn_pb_t_kernel(
         for i in range(X_BANKS):
             copy = nc.scalar.copy if i % 2 else nc.vector.tensor_copy
             sort_x(copy, 0, i, flip_x(0, i))
-        for b in range(PAIR):
-            quantise_x(0, b)
+        quantise_x(0, 0, slice(0, PANEL // 2))
+        quantise_x(0, 0, slice(PANEL // 2, PANEL))
+        quantise_x(0, 1)
 
         jobs = [(group, s, b) for group in range(GROUPS) for s in range(2) for b in range(PAIR)]
         assert len(jobs) == GROUPS * X_BANKS
-        quarters = len(jobs) * ROWS
-        staging = {}
-        hop1_grouped = {}
+        hop1_rows = {}
         hop1_quantised = {}
-        for n in range(quarters + LAG):
-            alone = n >= quarters - ROWS
-            if n < quarters:
-                job, j = divmod(n, ROWS)
-                group, s, b = jobs[job]
-                cols = slice(j * P, (j + 1) * P)
-                if j == 0:
-                    staging[1, job] = store_pool.tile([P, ROWS, NODES], F32, name="staged")
-                product_to_hbm(
-                    x_codes[group][:, b, cols],
-                    x_scales[group][:, b, cols],
-                    s,
-                    j,
-                    staging[1, job],
-                    hop1_outs[s],
-                    group,
-                    b,
-                    alone,
-                )
+        for n in range(len(jobs) + LAG):
+            if n < len(jobs):
+                group, s, b = jobs[n]
+                staged = store_pool.tile([P, ROWS, NODES], F32, name="staged")
+                hop1_rows[n] = []
+                for j in range(ROWS):
+                    cols = slice(j * P, (j + 1) * P)
+                    product_to_hbm(
+                        nc.scalar.copy,
+                        x_codes[group][:, b, cols],
+                        x_scales[group][:, b, cols],
+                        s,
+                        j,
+                        staged,
+                        hop1_outs[s],
+                        group,
+                        b,
+                        n == 0,
+                    )
+                    hop1_rows[n].append(round_hop1(staged, j))
+            if n == 0:
+                quantise_support(1)
+            flipped = flip_hop1(hop1_rows[n - 1]) if 1 <= n <= len(jobs) else None
+            more_x = n < len(jobs) and group + 1 < GROUPS
+            i = n % X_BANKS
+            if more_x:
+                if i == 0:
+                    new_group(group + 1)
+                x_bank = flip_x(group + 1, i)
+            if flipped:
+                grouped = group_hop1(flipped)
+            if more_x:
+                sort_x(nc.vector.tensor_copy, group + 1, i, x_bank)
+            if flipped:
+                hop1_quantised[n - 1] = quantise_hop1(grouped)
+            if more_x and i == X_BANKS - 1:
+                for next_b in range(PAIR):
+                    quantise_x(group + 1, next_b)
             if n >= LAG:
-                job, j = divmod(n - LAG, ROWS)
-                group, s, b = jobs[job]
+                group, s, b = jobs[n - LAG]
                 codes, scales = hop1_quantised[n - LAG]
-                if j == 0:
-                    staging[2, job] = store_pool.tile([P, ROWS, NODES], F32, name="staged")
-                product_to_hbm(
-                    codes[:], scales[:], s, j, staging[2, job], hop2_outs[s], group, b, alone
-                )
-            if n < quarters:
-                job, j = divmod(n, ROWS)
-                group, s, b = jobs[job]
-                hop1_grouped[n] = flipped_first_hop(group, s, b, j)
-            if 1 <= n <= quarters:
-                hop1_quantised[n - 1] = quantise_hop1(hop1_grouped[n - 1])
-            if n < quarters:
-                i = job % X_BANKS
-                if group + 1 < GROUPS and j == 0:
-                    if i == 0:
-                        new_group(group + 1)
-                    sort_x(nc.vector.tensor_copy, group + 1, i, flip_x(group + 1, i))
-                if group + 1 < GROUPS and i == X_BANKS - 1 and 1 <= j <= PAIR:
-                    quantise_x(group + 1, j - 1)
-                if n == ROWS - 1:
-                    quantise_support(1)
+                staged = store_pool.tile([P, ROWS, NODES], F32, name="staged")
+                for j in range(ROWS):
+                    cols = slice(j * P, (j + 1) * P)
+                    product_to_hbm(
+                        nc.vector.tensor_copy if j == ROWS - 1 else nc.scalar.copy,
+                        codes[:, cols],
+                        scales[:, cols],
+                        s,
+                        j,
+                        staged,
+                        hop2_outs[s],
+                        group,
+                        b,
+                        n == len(jobs) + LAG - 1,
+                    )

@@ -14,16 +14,18 @@ PACK = 4
 BATCHES, CHANNELS, NODES, STEPS = 4, 64, 512, 16
 assert NODES == P * PACK
 PAIR = P // CHANNELS
-
-ROWS = 4
-PANEL = P * ROWS
-PANEL_STEPS = PANEL // CHANNELS
-HALVES = STEPS // PANEL_STEPS
-PAIRS = BATCHES // PAIR
-GROUPS = PAIRS * HALVES
-X_BANKS = PANEL_STEPS // 2
 WORD_STEPS = STEPS // 2
-LAG = 2
+
+GROUPS = ((0, 0, 4), (0, 4, 4), (0, 8, 8), (1, 0, 8), (1, 8, 8))
+QB = 3
+XE = 12
+X0 = 6
+S1 = 3
+MM, MN = 2, 0
+VM, VN = 4, 1
+
+LAG = 10
+FLIP_LAG = 6
 
 FLOPS = 4 * 2 * BATCHES * STEPS * CHANNELS * NODES * NODES
 
@@ -39,12 +41,12 @@ def tile_adaptivegcn_pb_t_kernel(
     with ExitStack() as ctx:
         ctx.enter_context(tc.manual_schedule())
         resident = ctx.enter_context(tc.tile_pool(name="resident", bufs=1))
-        x_pool = ctx.enter_context(tc.tile_pool(name="x_pool", bufs=2))
-        hop1_pool = ctx.enter_context(tc.tile_pool(name="hop1_pool", bufs=LAG + 1))
-        rows_pool = ctx.enter_context(tc.tile_pool(name="rows_pool", bufs=2 * ROWS))
+        x_pool = ctx.enter_context(tc.tile_pool(name="x_pool", bufs=3))
+        hop1_pool = ctx.enter_context(tc.tile_pool(name="hop1_pool", bufs=8))
+        rows_pool = ctx.enter_context(tc.tile_pool(name="rows_pool", bufs=FLIP_LAG + 2))
         store_pool = ctx.enter_context(tc.tile_pool(name="store_pool", bufs=12))
-        psum_quant = ctx.enter_context(tc.psum_pool(name="psum_quant", bufs=3))
-        psum_store = ctx.enter_context(tc.psum_pool(name="psum_store", bufs=5))
+        psum_quant = ctx.enter_context(tc.psum_pool(name="psum_quant", bufs=QB))
+        psum_store = ctx.enter_context(tc.psum_pool(name="psum_store", bufs=8 - QB))
 
         def load_support(s):
             rows = resident.tile([P, PACK, NODES], BF16, name="support_rows_%d" % s)
@@ -66,11 +68,13 @@ def tile_adaptivegcn_pb_t_kernel(
 
         ident_f32 = resident.tile([P, P], F32)
         make_identity(nc, ident_f32[:])
-        sort_channels = resident.tile([P, P], F32)
-        nc.vector.tensor_copy(
-            out=sort_channels[:].rearrange("q (b j c) -> q b j c", j=ROWS, b=PAIR),
-            in_=ident_f32[:].rearrange("q (b c j) -> q b j c", j=ROWS, b=PAIR),
-        )
+        sort_channels = {}
+        for rows in (2, 4):
+            sort_channels[rows] = resident.tile([P, P], F32, name="sort_channels_%d" % rows)
+            nc.vector.tensor_copy(
+                out=sort_channels[rows][:].rearrange("q (b j c) -> q b j c", j=rows, b=PAIR),
+                in_=ident_f32[:].rearrange("q (b c j) -> q b j c", j=rows, b=PAIR),
+            )
 
         support_codes = {}
         support_scales = {}
@@ -110,35 +114,40 @@ def tile_adaptivegcn_pb_t_kernel(
         x_scales = {}
 
         def new_group(group):
+            panel = GROUPS[group][2] * CHANNELS
             x_grouped[group] = x_pool.tile(
-                [P, PAIR, PANEL * PACK], BF16, name="x_grouped", align_bytes=64
+                [P, PAIR, panel * PACK], BF16, name="x_grouped", align_bytes=64
             )
-            x_codes[group] = x_pool.tile([P, PAIR, PANEL], U32, name="x_codes", align_bytes=64)
-            x_scales[group] = x_pool.tile([P, PAIR, PANEL], U8, name="x_scales", align_bytes=64)
+            x_codes[group] = x_pool.tile([P, PAIR, panel], U32, name="x_codes", align_bytes=64)
+            x_scales[group] = x_pool.tile([P, PAIR, panel], U8, name="x_scales", align_bytes=64)
 
         def flip_x(group, i):
-            pair, half = divmod(group, HALVES)
+            pair, first, steps = GROUPS[group]
             bank = psum_quant.tile([P, PACK, P], F32, name="x_flipped", tag="quant_bank")
             words = x_rows[pair][:].bitcast(F32).rearrange("r (k w) -> r k w", w=WORD_STEPS)
             for t in range(PACK):
                 nc.tensor.transpose(
-                    bank[:, t, :], words[:, t::PACK, half * X_BANKS + i], sort_channels[:]
+                    bank[:, t, :], words[:, t::PACK, first // 2 + i], sort_channels[steps // 2][:]
                 )
             return bank
 
         def sort_x(copy, group, i, bank):
-            halves = bank[:].bitcast(BF16).rearrange("p t (bj c e) -> p e bj c t", e=2, c=P // (PAIR * ROWS))
+            steps = GROUPS[group][2]
+            rows = steps // 2
+            halves = bank[:].bitcast(BF16).rearrange(
+                "p t (bj c e) -> p e bj c t", e=2, bj=PAIR * rows
+            )
             sorted_steps = x_grouped[group][:].rearrange(
-                "p b (j i e c t) -> p i e (b j) c t", j=ROWS, i=X_BANKS, e=2, t=PACK
+                "p b (j i e c t) -> p i e (b j) c t", j=rows, i=steps // 2, e=2, t=PACK
             )
             for e in range(2):
                 copy(out=sorted_steps[:, i, e], in_=halves[:, e])
 
-        def quantise_x(group, b, cols=slice(0, PANEL)):
+        def quantise_x(group, b):
             nc.vector.quantize_mx(
-                out=x_codes[group][:, b, cols].bitcast(FP8X4),
-                scales=x_scales[group][:, b, cols],
-                in_=x_grouped[group][:, b, cols.start * PACK : cols.stop * PACK],
+                out=x_codes[group][:, b, :].bitcast(FP8X4),
+                scales=x_scales[group][:, b, :],
+                in_=x_grouped[group][:, b, :],
             )
 
         def product_to_hbm(copy, codes, scales, s, j, staged, out, group, b, alone):
@@ -156,12 +165,13 @@ def tile_adaptivegcn_pb_t_kernel(
                 out=staged[:, j, :].rearrange("p (m t) -> p m t", t=PACK),
                 in_=bank[:].rearrange("p (t m) -> p m t", t=PACK),
             )
-            pair, half = divmod(group, HALVES)
-            first = (pair * PAIR + b) * STEPS + half * PANEL_STEPS
-            in_hbm = out[first : first + PANEL_STEPS].rearrange("l (c j) w -> (l c) j w", j=ROWS)
+            pair, first, steps = GROUPS[group]
+            n = (pair * PAIR + b) * STEPS + first
+            rows = steps // 2
+            in_hbm = out[n : n + steps].rearrange("l (c j) w -> (l c) j w", j=rows)
             if alone:
                 nc.sync.dma_start(out=in_hbm[:, j, :], in_=staged[:, j, :])
-            elif j == ROWS - 1:
+            elif j == rows - 1:
                 nc.sync.dma_start(out=in_hbm, in_=staged[:])
 
         def round_hop1(staged, j):
@@ -176,34 +186,53 @@ def tile_adaptivegcn_pb_t_kernel(
             )
             return rows
 
-        def flip_hop1(quarter_rows):
-            banks = []
-            for half in range(2):
-                bank = psum_quant.tile([P, 2, 2, P], F32, name="hop1_flipped", tag="quant_bank")
-                for i in range(2):
-                    words = quarter_rows[2 * half + i][:].bitcast(F32)
-                    for u in range(2):
-                        nc.tensor.transpose(
-                            bank[:, i, u, :], words[:, u * P : (u + 1) * P], ident_f32[:]
-                        )
-                banks.append(bank)
-            return banks
+        def flip_hop1(slices):
+            bank = psum_quant.tile([P, 2, 2, P], F32, name="hop1_flipped", tag="quant_bank")
+            for i in range(2):
+                words = slices[i][:].bitcast(F32)
+                for u in range(2):
+                    nc.tensor.transpose(
+                        bank[:, i, u, :], words[:, u * P : (u + 1) * P], ident_f32[:]
+                    )
+            return bank
 
-        def group_hop1(banks):
-            grouped = hop1_pool.tile([P, PANEL * PACK], BF16, name="hop1_grouped", align_bytes=64)
-            words = grouped[:].bitcast(F32)
-            for half, bank in enumerate(banks):
-                nc.vector.tensor_copy(
-                    out=words[:, half * NODES : (half + 1) * NODES].rearrange(
-                        "p (i r u) -> p i r u", i=2, u=2
-                    ),
-                    in_=bank[:].rearrange("p i u r -> p i r u"),
+        def multiply_flipped(n):
+            g, s, b, j = slices[n]
+            cols = slice(j * P, (j + 1) * P)
+            bank = psum_quant.tile([P, PACK, P], F32, name="hop1_multiplied", tag="quant_bank")
+            for t in range(PACK):
+                nodes = slice(t * P, (t + 1) * P)
+                nc.tensor.matmul_mx(
+                    out=bank[:, t, :],
+                    lhsT=support_codes[s][:, nodes].bitcast(FP8X4),
+                    lhsT_scale=support_scales[s][:, nodes],
+                    rhs=x_codes[g][:, b, cols].bitcast(FP8X4),
+                    rhs_scale=x_scales[g][:, b, cols],
+                    start=True,
+                    stop=True,
                 )
+            return bank
+
+        def group_multiplied(grouped, i, bank):
+            nc.vector.tensor_copy(
+                out=grouped[:, i * NODES : (i + 1) * NODES].rearrange("p (r t) -> p r t", t=PACK),
+                in_=bank[:].rearrange("p t r -> p r t"),
+            )
+
+        def new_grouped():
+            return hop1_pool.tile([P, 2 * NODES], BF16, name="hop1_grouped", align_bytes=64)
+
+        def group_hop1(bank):
+            grouped = new_grouped()
+            nc.vector.tensor_copy(
+                out=grouped[:].bitcast(F32).rearrange("p (i r u) -> p i r u", i=2, u=2),
+                in_=bank[:].rearrange("p i u r -> p i r u"),
+            )
             return grouped
 
         def quantise_hop1(grouped):
-            codes = hop1_pool.tile([P, PANEL], U32, name="hop1_codes", align_bytes=64)
-            scales = hop1_pool.tile([P, PANEL], U8, name="hop1_scales", align_bytes=64)
+            codes = hop1_pool.tile([P, 2 * P], U32, name="hop1_codes", align_bytes=64)
+            scales = hop1_pool.tile([P, 2 * P], U8, name="hop1_scales", align_bytes=64)
             nc.vector.quantize_mx(
                 out=codes[:].bitcast(FP8X4), scales=scales[:], in_=grouped[:]
             )
@@ -211,70 +240,94 @@ def tile_adaptivegcn_pb_t_kernel(
 
         quantise_support(0)
         new_group(0)
-        for i in range(X_BANKS):
-            copy = nc.scalar.copy if i % 2 else nc.vector.tensor_copy
-            sort_x(copy, 0, i, flip_x(0, i))
-        quantise_x(0, 0, slice(0, PANEL // 2))
-        quantise_x(0, 0, slice(PANEL // 2, PANEL))
-        quantise_x(0, 1)
+        new_group(1)
+        first_banks = [(g, i, flip_x(g, i)) for g in range(2) for i in range(2)]
+        for g, i, bank in first_banks[:2]:
+            sort_x(nc.scalar.copy if i % 2 else nc.vector.tensor_copy, g, i, bank)
+        for b in range(PAIR):
+            quantise_x(0, b)
+        for g, i, bank in first_banks[2:]:
+            sort_x(nc.vector.tensor_copy, g, i, bank)
+        for b in range(PAIR):
+            quantise_x(1, b)
 
-        jobs = [(group, s, b) for group in range(GROUPS) for s in range(2) for b in range(PAIR)]
-        assert len(jobs) == GROUPS * X_BANKS
+        slices = [
+            (g, s, b, j)
+            for block in ((0, 1), (2,), (3,), (4,))
+            for s in range(2)
+            for g in block
+            for b in range(PAIR)
+            for j in range(GROUPS[g][2] // 2)
+        ]
+        x_banks = [(g, i) for g in range(2, len(GROUPS)) for i in range(GROUPS[g][2] // 2)]
+        x_ready = []
+        staging = {}
         hop1_rows = {}
+        hop1_grouped = {}
         hop1_quantised = {}
-        for n in range(len(jobs) + LAG):
-            if n < len(jobs):
-                group, s, b = jobs[n]
-                staged = store_pool.tile([P, ROWS, NODES], F32, name="staged")
-                hop1_rows[n] = []
-                for j in range(ROWS):
-                    cols = slice(j * P, (j + 1) * P)
-                    product_to_hbm(
-                        nc.scalar.copy,
-                        x_codes[group][:, b, cols],
-                        x_scales[group][:, b, cols],
-                        s,
-                        j,
-                        staged,
-                        hop1_outs[s],
-                        group,
-                        b,
-                        n == 0,
-                    )
-                    hop1_rows[n].append(round_hop1(staged, j))
-            if n == 0:
-                quantise_support(1)
-            flipped = flip_hop1(hop1_rows[n - 1]) if 1 <= n <= len(jobs) else None
-            more_x = n < len(jobs) and group + 1 < GROUPS
-            i = n % X_BANKS
-            if more_x:
-                if i == 0:
-                    new_group(group + 1)
-                x_bank = flip_x(group + 1, i)
-            if flipped:
-                grouped = group_hop1(flipped)
-            if more_x:
-                sort_x(nc.vector.tensor_copy, group + 1, i, x_bank)
-            if flipped:
-                hop1_quantised[n - 1] = quantise_hop1(grouped)
-            if more_x and i == X_BANKS - 1:
-                for next_b in range(PAIR):
-                    quantise_x(group + 1, next_b)
+
+        def multiplied(n):
+            return n // 2 % MM < MN
+
+        def product(hop, n, copy, codes, scales, alone):
+            g, s, b, j = slices[n]
+            if j == 0:
+                rows = GROUPS[g][2] // 2
+                staging[hop] = store_pool.tile([P, rows, NODES], F32, name="staged")
+            outs = hop1_outs if hop == 1 else hop2_outs
+            product_to_hbm(copy, codes, scales, s, j, staging[hop], outs[s], g, b, alone)
+
+        for n in range(len(slices) + LAG):
+            if n < len(slices):
+                g, s, b, j = slices[n]
+                cols = slice(j * P, (j + 1) * P)
+                by_vector = False
+                product(
+                    1,
+                    n,
+                    nc.vector.tensor_copy if by_vector else nc.scalar.copy,
+                    x_codes[g][:, b, cols],
+                    x_scales[g][:, b, cols],
+                    n < 2,
+                )
+                if not multiplied(n):
+                    hop1_rows[n] = round_hop1(staging[1], j)
             if n >= LAG:
-                group, s, b = jobs[n - LAG]
-                codes, scales = hop1_quantised[n - LAG]
-                staged = store_pool.tile([P, ROWS, NODES], F32, name="staged")
-                for j in range(ROWS):
-                    cols = slice(j * P, (j + 1) * P)
-                    product_to_hbm(
-                        nc.vector.tensor_copy if j == ROWS - 1 else nc.scalar.copy,
-                        codes[:, cols],
-                        scales[:, cols],
-                        s,
-                        j,
-                        staged,
-                        hop2_outs[s],
-                        group,
-                        b,
-                        n == len(jobs) + LAG - 1,
-                    )
+                codes, scales = hop1_quantised[(n - LAG) // 2]
+                cols = slice((n - LAG) % 2 * P, ((n - LAG) % 2 + 1) * P)
+                by_vector = (n - LAG) % VM < VN
+                product(
+                    2,
+                    n - LAG,
+                    nc.vector.tensor_copy if by_vector else nc.scalar.copy,
+                    codes[:, cols],
+                    scales[:, cols],
+                    n >= len(slices) + LAG - 4,
+                )
+            if n == S1:
+                quantise_support(1)
+            if n % 2 == 0:
+                if FLIP_LAG <= n < len(slices) + FLIP_LAG:
+                    k = n - FLIP_LAG
+                    if multiplied(k):
+                        grouped = new_grouped()
+                        banks = [multiply_flipped(k + i) for i in range(2)]
+                        for i in range(2):
+                            group_multiplied(grouped, i, banks[i])
+                        hop1_grouped[k // 2] = grouped
+                    else:
+                        bank = flip_hop1((hop1_rows[k], hop1_rows[k + 1]))
+                        hop1_grouped[k // 2] = group_hop1(bank)
+                if x_banks and n >= X0 and (n % 4 == 2 or n <= XE):
+                    g, i = x_banks.pop(0)
+                    if i == 0:
+                        new_group(g)
+                    sort_x(nc.scalar.copy if n <= XE and i % 2 else nc.vector.tensor_copy, g, i, flip_x(g, i))
+                    if i == GROUPS[g][2] // 2 - 1:
+                        x_ready.extend((g, b) for b in range(PAIR))
+            else:
+                if FLIP_LAG <= n < len(slices) + FLIP_LAG:
+                    k = (n - 1 - FLIP_LAG) // 2
+                    hop1_quantised[k] = quantise_hop1(hop1_grouped[k])
+                if x_ready:
+                    quantise_x(*x_ready.pop(0))

@@ -18,11 +18,16 @@ WORD_STEPS = STEPS // 2
 
 GROUPS = ((0, 0, 4), (0, 4, 4), (0, 8, 8), (1, 0, 8), (1, 8, 8))
 QB = 3
+VE = 0
+SX = 1
 XE = 12
 X0 = 6
 S1 = 3
 MM, MN = 2, 0
-VM, VN = 4, 1
+VM, VR = 4, 3
+EM = 0
+QUAD = 2
+TA = 2
 
 LAG = 10
 FLIP_LAG = 6
@@ -42,7 +47,7 @@ def tile_adaptivegcn_pb_t_kernel(
         ctx.enter_context(tc.manual_schedule())
         resident = ctx.enter_context(tc.tile_pool(name="resident", bufs=1))
         x_pool = ctx.enter_context(tc.tile_pool(name="x_pool", bufs=3))
-        hop1_pool = ctx.enter_context(tc.tile_pool(name="hop1_pool", bufs=8))
+        hop1_pool = ctx.enter_context(tc.tile_pool(name="hop1_pool", bufs=16 // QUAD + 1))
         rows_pool = ctx.enter_context(tc.tile_pool(name="rows_pool", bufs=FLIP_LAG + 2))
         store_pool = ctx.enter_context(tc.tile_pool(name="store_pool", bufs=12))
         psum_quant = ctx.enter_context(tc.psum_pool(name="psum_quant", bufs=QB))
@@ -220,19 +225,18 @@ def tile_adaptivegcn_pb_t_kernel(
             )
 
         def new_grouped():
-            return hop1_pool.tile([P, 2 * NODES], BF16, name="hop1_grouped", align_bytes=64)
+            return hop1_pool.tile([P, QUAD * NODES], BF16, name="hop1_grouped", align_bytes=64)
 
-        def group_hop1(bank):
-            grouped = new_grouped()
+        def group_hop1(grouped, first, bank):
+            words = grouped[:].bitcast(F32).rearrange("p (i r u) -> p i r u", i=QUAD, u=2)
             nc.vector.tensor_copy(
-                out=grouped[:].bitcast(F32).rearrange("p (i r u) -> p i r u", i=2, u=2),
+                out=words[:, first : first + 2],
                 in_=bank[:].rearrange("p i u r -> p i r u"),
             )
-            return grouped
 
         def quantise_hop1(grouped):
-            codes = hop1_pool.tile([P, 2 * P], U32, name="hop1_codes", align_bytes=64)
-            scales = hop1_pool.tile([P, 2 * P], U8, name="hop1_scales", align_bytes=64)
+            codes = hop1_pool.tile([P, QUAD * P], U32, name="hop1_codes", align_bytes=64)
+            scales = hop1_pool.tile([P, QUAD * P], U8, name="hop1_scales", align_bytes=64)
             nc.vector.quantize_mx(
                 out=codes[:].bitcast(FP8X4), scales=scales[:], in_=grouped[:]
             )
@@ -267,7 +271,7 @@ def tile_adaptivegcn_pb_t_kernel(
         hop1_quantised = {}
 
         def multiplied(n):
-            return n // 2 % MM < MN
+            return n // 2 % MM < MN or n < EM
 
         def product(hop, n, copy, codes, scales, alone):
             g, s, b, j = slices[n]
@@ -281,7 +285,7 @@ def tile_adaptivegcn_pb_t_kernel(
             if n < len(slices):
                 g, s, b, j = slices[n]
                 cols = slice(j * P, (j + 1) * P)
-                by_vector = False
+                by_vector = n < VE and n % 2 == 1
                 product(
                     1,
                     n,
@@ -293,9 +297,9 @@ def tile_adaptivegcn_pb_t_kernel(
                 if not multiplied(n):
                     hop1_rows[n] = round_hop1(staging[1], j)
             if n >= LAG:
-                codes, scales = hop1_quantised[(n - LAG) // 2]
-                cols = slice((n - LAG) % 2 * P, ((n - LAG) % 2 + 1) * P)
-                by_vector = (n - LAG) % VM < VN
+                codes, scales = hop1_quantised[(n - LAG) // QUAD]
+                cols = slice((n - LAG) % QUAD * P, ((n - LAG) % QUAD + 1) * P)
+                by_vector = (n - LAG) % VM == VR or n >= len(slices) and n % TA == 1
                 product(
                     2,
                     n - LAG,
@@ -309,25 +313,26 @@ def tile_adaptivegcn_pb_t_kernel(
             if n % 2 == 0:
                 if FLIP_LAG <= n < len(slices) + FLIP_LAG:
                     k = n - FLIP_LAG
+                    if k % QUAD == 0:
+                        hop1_grouped[k // QUAD] = new_grouped()
+                    grouped = hop1_grouped[k // QUAD]
                     if multiplied(k):
-                        grouped = new_grouped()
                         banks = [multiply_flipped(k + i) for i in range(2)]
                         for i in range(2):
-                            group_multiplied(grouped, i, banks[i])
-                        hop1_grouped[k // 2] = grouped
+                            group_multiplied(grouped, k % QUAD + i, banks[i])
                     else:
-                        bank = flip_hop1((hop1_rows[k], hop1_rows[k + 1]))
-                        hop1_grouped[k // 2] = group_hop1(bank)
+                        group_hop1(grouped, k % QUAD, flip_hop1((hop1_rows[k], hop1_rows[k + 1])))
                 if x_banks and n >= X0 and (n % 4 == 2 or n <= XE):
                     g, i = x_banks.pop(0)
                     if i == 0:
                         new_group(g)
-                    sort_x(nc.scalar.copy if n <= XE and i % 2 else nc.vector.tensor_copy, g, i, flip_x(g, i))
+                    sort_x(nc.scalar.copy if n <= XE and i % 4 >= 4 - SX else nc.vector.tensor_copy, g, i, flip_x(g, i))
                     if i == GROUPS[g][2] // 2 - 1:
                         x_ready.extend((g, b) for b in range(PAIR))
             else:
                 if FLIP_LAG <= n < len(slices) + FLIP_LAG:
-                    k = (n - 1 - FLIP_LAG) // 2
-                    hop1_quantised[k] = quantise_hop1(hop1_grouped[k])
+                    k = n - FLIP_LAG
+                    if k % QUAD == QUAD - 1:
+                        hop1_quantised[k // QUAD] = quantise_hop1(hop1_grouped[k // QUAD])
                 if x_ready:
                     quantise_x(*x_ready.pop(0))

@@ -19,10 +19,10 @@ WORD_STEPS = STEPS // 2
 GROUPS = ((0, 0, 4), (0, 4, 4), (0, 8, 8), (1, 0, 8), (1, 8, 8))
 QB = 3
 VE = 0
-SX = 1
+SX = 2
 XE = 12
 X0 = 6
-S1 = 3
+S1 = 2
 MM, MN = 2, 0
 VM, VR = 4, 3
 EM = 0
@@ -66,9 +66,8 @@ def tile_adaptivegcn_pb_t_kernel(
                 nc.sync.dma_start(out=tile[:, cols], in_=rows[:, cols])
             return tile
 
-        support_rows = {0: load_support(0)}
         x_rows = {0: load_x(0)}
-        support_rows[1] = load_support(1)
+        support_rows = {s: load_support(s) for s in range(2)}
         x_rows[1] = load_x(1)
 
         ident_f32 = resident.tile([P, P], F32)
@@ -84,23 +83,25 @@ def tile_adaptivegcn_pb_t_kernel(
         support_codes = {}
         support_scales = {}
 
-        def quantise_support(s):
+        def group_support(s, engines):
             grouped = resident.tile(
                 [P, NODES, PACK], BF16, name="support_grouped_%d" % s, align_bytes=64
             )
             words = grouped[:].rearrange("p w k -> p (w k)").bitcast(F32)
+            halves = []
             for half in range(2):
                 flipped = psum_store.tile([P, 2, 2, P], F32, tag="store_bank")
                 for i in range(2):
                     row = support_rows[s][:, 2 * half + i, :].bitcast(F32)
                     for u in range(2):
                         nc.tensor.transpose(flipped[:, i, u, :], row[:, u::2], ident_f32[:])
-                copy = nc.vector.tensor_copy if half == 0 else nc.scalar.copy
+                halves.append(flipped)
+            for half, copy in enumerate(engines):
                 copy(
                     out=words[:, half * NODES : (half + 1) * NODES].rearrange(
                         "p (i m u) -> p i m u", i=2, u=2
                     ),
-                    in_=flipped[:].rearrange("p i u m -> p i m u"),
+                    in_=halves[half][:].rearrange("p i u m -> p i m u"),
                 )
             support_codes[s] = resident.tile(
                 [P, NODES], U32, name="support_codes_%d" % s, align_bytes=64
@@ -108,6 +109,9 @@ def tile_adaptivegcn_pb_t_kernel(
             support_scales[s] = resident.tile(
                 [P, NODES], U8, name="support_scales_%d" % s, align_bytes=64
             )
+            return grouped
+
+        def quantise_support(s, grouped):
             nc.vector.quantize_mx(
                 out=support_codes[s][:].bitcast(FP8X4),
                 scales=support_scales[s][:],
@@ -242,16 +246,19 @@ def tile_adaptivegcn_pb_t_kernel(
             )
             return codes, scales
 
-        quantise_support(0)
+        S1E = (nc.vector.tensor_copy, nc.scalar.copy)
+        engines = (nc.vector.tensor_copy, nc.scalar.copy)
         new_group(0)
         new_group(1)
-        first_banks = [(g, i, flip_x(g, i)) for g in range(2) for i in range(2)]
-        for g, i, bank in first_banks[:2]:
-            sort_x(nc.scalar.copy if i % 2 else nc.vector.tensor_copy, g, i, bank)
+        first_banks = [flip_x(0, i) for i in range(2)]
+        for i in range(2):
+            sort_x(engines[i], 0, i, first_banks[i])
+        grouped_support = group_support(0, engines)
         for b in range(PAIR):
             quantise_x(0, b)
-        for g, i, bank in first_banks[2:]:
-            sort_x(nc.vector.tensor_copy, g, i, bank)
+        quantise_support(0, grouped_support)
+        for i in range(2):
+            sort_x(engines[1 - i], 1, i, flip_x(1, i))
         for b in range(PAIR):
             quantise_x(1, b)
 
@@ -309,7 +316,7 @@ def tile_adaptivegcn_pb_t_kernel(
                     n >= len(slices) + LAG - 4,
                 )
             if n == S1:
-                quantise_support(1)
+                quantise_support(1, group_support(1, S1E))
             if n % 2 == 0:
                 if FLIP_LAG <= n < len(slices) + FLIP_LAG:
                     k = n - FLIP_LAG

@@ -23,7 +23,7 @@ SX = 2
 XE = 12
 X0 = 6
 S1 = 2
-MM, MN = 2, 0
+MM, MN = 8, 1
 VM, VR = 4, 3
 EM = 0
 QUAD = 2
@@ -278,7 +278,7 @@ def tile_adaptivegcn_pb_t_kernel(
         hop1_quantised = {}
 
         def multiplied(n):
-            return n // 2 % MM < MN or n < EM
+            return n // 2 % MM >= MM - MN
 
         def product(hop, n, copy, codes, scales, alone):
             g, s, b, j = slices[n]

from contextlib import ExitStack

import concourse.mybir as mybir
from concourse.masks import make_identity

BF16 = mybir.dt.bfloat16
F32 = mybir.dt.float32
U32 = mybir.dt.uint32
U8 = mybir.dt.uint8
FP8X4 = mybir.dt.float8_e4m3fn_x4

P = 128
PACK = 4
BATCHES, CHANNELS, NODES, STEPS = 4, 64, 512, 16
assert NODES == P * PACK
PAIR = P // CHANNELS
WORD_STEPS = STEPS // 2

GROUPS = ((0, 0, 4), (0, 4, 4), (0, 8, 8), (1, 0, 8), (1, 8, 8))
QB = 3
VE = 0
SX = 2
XE = 12
X0 = 6
S1 = 2
MM, MN = 8, 1
VM, VR = 4, 3
EM = 0
QUAD = 2
TA = 2

LAG = 10
FLIP_LAG = 6

FLOPS = 4 * 2 * BATCHES * STEPS * CHANNELS * NODES * NODES


def tile_adaptivegcn_pb_t_kernel(
    tc, x, support0, support1, out_0, out_1, out_2, out_3
):
    nc = tc.nc
    supports = (support0, support1)
    hop1_outs = (out_0, out_2)
    hop2_outs = (out_1, out_3)

    with ExitStack() as ctx:
        ctx.enter_context(tc.manual_schedule())
        resident = ctx.enter_context(tc.tile_pool(name="resident", bufs=1))
        x_pool = ctx.enter_context(tc.tile_pool(name="x_pool", bufs=3))
        hop1_pool = ctx.enter_context(tc.tile_pool(name="hop1_pool", bufs=16 // QUAD + 1))
        rows_pool = ctx.enter_context(tc.tile_pool(name="rows_pool", bufs=FLIP_LAG + 2))
        store_pool = ctx.enter_context(tc.tile_pool(name="store_pool", bufs=12))
        psum_quant = ctx.enter_context(tc.psum_pool(name="psum_quant", bufs=QB))
        psum_store = ctx.enter_context(tc.psum_pool(name="psum_store", bufs=8 - QB))

        def load_support(s):
            rows = resident.tile([P, PACK, NODES], BF16, name="support_rows_%d" % s)
            nc.sync.dma_start(out=rows[:], in_=supports[s].rearrange("(p t) v -> p t v", t=PACK))
            return rows

        def load_x(pair):
            rows = x.rearrange("b c f -> (b c) f")[pair * P : (pair + 1) * P]
            tile = resident.tile([P, NODES * STEPS], BF16, name="x_rows_%d" % pair)
            for u in range(2):
                cols = slice(u * NODES * STEPS // 2, (u + 1) * NODES * STEPS // 2)
                nc.sync.dma_start(out=tile[:, cols], in_=rows[:, cols])
            return tile

        x_rows = {0: load_x(0)}
        support_rows = {s: load_support(s) for s in range(2)}
        x_rows[1] = load_x(1)

        ident_f32 = resident.tile([P, P], F32)
        make_identity(nc, ident_f32[:])
        sort_channels = {}
        for rows in (2, 4):
            sort_channels[rows] = resident.tile([P, P], F32, name="sort_channels_%d" % rows)
            nc.vector.tensor_copy(
                out=sort_channels[rows][:].rearrange("q (b j c) -> q b j c", j=rows, b=PAIR),
                in_=ident_f32[:].rearrange("q (b c j) -> q b j c", j=rows, b=PAIR),
            )

        support_codes = {}
        support_scales = {}

        def group_support(s, engines):
            grouped = resident.tile(
                [P, NODES, PACK], BF16, name="support_grouped_%d" % s, align_bytes=64
            )
            words = grouped[:].rearrange("p w k -> p (w k)").bitcast(F32)
            halves = []
            for half in range(2):
                flipped = psum_store.tile([P, 2, 2, P], F32, tag="store_bank")
                for i in range(2):
                    row = support_rows[s][:, 2 * half + i, :].bitcast(F32)
                    for u in range(2):
                        nc.tensor.transpose(flipped[:, i, u, :], row[:, u::2], ident_f32[:])
                halves.append(flipped)
            for half, copy in enumerate(engines):
                copy(
                    out=words[:, half * NODES : (half + 1) * NODES].rearrange(
                        "p (i m u) -> p i m u", i=2, u=2
                    ),
                    in_=halves[half][:].rearrange("p i u m -> p i m u"),
                )
            support_codes[s] = resident.tile(
                [P, NODES], U32, name="support_codes_%d" % s, align_bytes=64
            )
            support_scales[s] = resident.tile(
                [P, NODES], U8, name="support_scales_%d" % s, align_bytes=64
            )
            return grouped

        def quantise_support(s, grouped):
            nc.vector.quantize_mx(
                out=support_codes[s][:].bitcast(FP8X4),
                scales=support_scales[s][:],
                in_=grouped[:].rearrange("p w t -> p (w t)"),
            )

        x_grouped = {}
        x_codes = {}
        x_scales = {}

        def new_group(group):
            panel = GROUPS[group][2] * CHANNELS
            x_grouped[group] = x_pool.tile(
                [P, PAIR, panel * PACK], BF16, name="x_grouped", align_bytes=64
            )
            x_codes[group] = x_pool.tile([P, PAIR, panel], U32, name="x_codes", align_bytes=64)
            x_scales[group] = x_pool.tile([P, PAIR, panel], U8, name="x_scales", align_bytes=64)

        def flip_x(group, i):
            pair, first, steps = GROUPS[group]
            bank = psum_quant.tile([P, PACK, P], F32, name="x_flipped", tag="quant_bank")
            words = x_rows[pair][:].bitcast(F32).rearrange("r (k w) -> r k w", w=WORD_STEPS)
            for t in range(PACK):
                nc.tensor.transpose(
                    bank[:, t, :], words[:, t::PACK, first // 2 + i], sort_channels[steps // 2][:]
                )
            return bank

        def sort_x(copy, group, i, bank):
            steps = GROUPS[group][2]
            rows = steps // 2
            halves = bank[:].bitcast(BF16).rearrange(
                "p t (bj c e) -> p e bj c t", e=2, bj=PAIR * rows
            )
            sorted_steps = x_grouped[group][:].rearrange(
                "p b (j i e c t) -> p i e (b j) c t", j=rows, i=steps // 2, e=2, t=PACK
            )
            for e in range(2):
                copy(out=sorted_steps[:, i, e], in_=halves[:, e])

        def quantise_x(group, b):
            nc.vector.quantize_mx(
                out=x_codes[group][:, b, :].bitcast(FP8X4),
                scales=x_scales[group][:, b, :],
                in_=x_grouped[group][:, b, :],
            )

        def product_to_hbm(copy, codes, scales, s, j, staged, out, group, b, alone):
            bank = psum_store.tile([P, NODES], F32, tag="store_bank")
            nc.tensor.matmul_mx(
                out=bank[:],
                lhsT=codes.bitcast(FP8X4),
                lhsT_scale=scales,
                rhs=support_codes[s][:].bitcast(FP8X4),
                rhs_scale=support_scales[s][:],
                start=True,
                stop=True,
            )
            copy(
                out=staged[:, j, :].rearrange("p (m t) -> p m t", t=PACK),
                in_=bank[:].rearrange("p (t m) -> p m t", t=PACK),
            )
            pair, first, steps = GROUPS[group]
            n = (pair * PAIR + b) * STEPS + first
            rows = steps // 2
            in_hbm = out[n : n + steps].rearrange("l (c j) w -> (l c) j w", j=rows)
            if alone:
                nc.sync.dma_start(out=in_hbm[:, j, :], in_=staged[:, j, :])
            elif j == rows - 1:
                nc.sync.dma_start(out=in_hbm, in_=staged[:])

        def round_hop1(staged, j):
            rows = rows_pool.tile([P, NODES], BF16, name="hop1_rows")
            nc.gpsimd.tensor_scalar(
                out=rows[:].rearrange("r (u m e) -> r u m e", u=2, e=2),
                in0=staged[:, j, :].rearrange("r (m u e) -> r u m e", u=2, e=2),
                scalar1=1.0,
                scalar2=0.0,
                op0=mybir.AluOpType.mult,
                op1=mybir.AluOpType.add,
            )
            return rows

        def flip_hop1(slices):
            bank = psum_quant.tile([P, 2, 2, P], F32, name="hop1_flipped", tag="quant_bank")
            for i in range(2):
                words = slices[i][:].bitcast(F32)
                for u in range(2):
                    nc.tensor.transpose(
                        bank[:, i, u, :], words[:, u * P : (u + 1) * P], ident_f32[:]
                    )
            return bank

        def multiply_flipped(n):
            g, s, b, j = slices[n]
            cols = slice(j * P, (j + 1) * P)
            bank = psum_quant.tile([P, PACK, P], F32, name="hop1_multiplied", tag="quant_bank")
            for t in range(PACK):
                nodes = slice(t * P, (t + 1) * P)
                nc.tensor.matmul_mx(
                    out=bank[:, t, :],
                    lhsT=support_codes[s][:, nodes].bitcast(FP8X4),
                    lhsT_scale=support_scales[s][:, nodes],
                    rhs=x_codes[g][:, b, cols].bitcast(FP8X4),
                    rhs_scale=x_scales[g][:, b, cols],
                    start=True,
                    stop=True,
                )
            return bank

        def group_multiplied(grouped, i, bank):
            nc.vector.tensor_copy(
                out=grouped[:, i * NODES : (i + 1) * NODES].rearrange("p (r t) -> p r t", t=PACK),
                in_=bank[:].rearrange("p t r -> p r t"),
            )

        def new_grouped():
            return hop1_pool.tile([P, QUAD * NODES], BF16, name="hop1_grouped", align_bytes=64)

        def group_hop1(grouped, first, bank):
            words = grouped[:].bitcast(F32).rearrange("p (i r u) -> p i r u", i=QUAD, u=2)
            nc.vector.tensor_copy(
                out=words[:, first : first + 2],
                in_=bank[:].rearrange("p i u r -> p i r u"),
            )

        def quantise_hop1(grouped):
            codes = hop1_pool.tile([P, QUAD * P], U32, name="hop1_codes", align_bytes=64)
            scales = hop1_pool.tile([P, QUAD * P], U8, name="hop1_scales", align_bytes=64)
            nc.vector.quantize_mx(
                out=codes[:].bitcast(FP8X4), scales=scales[:], in_=grouped[:]
            )
            return codes, scales

        S1E = (nc.vector.tensor_copy, nc.scalar.copy)
        engines = (nc.vector.tensor_copy, nc.scalar.copy)
        new_group(0)
        new_group(1)
        first_banks = [flip_x(0, i) for i in range(2)]
        for i in range(2):
            sort_x(engines[i], 0, i, first_banks[i])
        grouped_support = group_support(0, engines)
        for b in range(PAIR):
            quantise_x(0, b)
        quantise_support(0, grouped_support)
        for i in range(2):
            sort_x(engines[1 - i], 1, i, flip_x(1, i))
        for b in range(PAIR):
            quantise_x(1, b)

        slices = [
            (g, s, b, j)
            for block in ((0, 1), (2,), (3,), (4,))
            for s in range(2)
            for g in block
            for b in range(PAIR)
            for j in range(GROUPS[g][2] // 2)
        ]
        x_banks = [(g, i) for g in range(2, len(GROUPS)) for i in range(GROUPS[g][2] // 2)]
        x_ready = []
        staging = {}
        hop1_rows = {}
        hop1_grouped = {}
        hop1_quantised = {}

        def multiplied(n):
            return n // 2 % MM >= MM - MN

        def product(hop, n, copy, codes, scales, alone):
            g, s, b, j = slices[n]
            if j == 0:
                rows = GROUPS[g][2] // 2
                staging[hop] = store_pool.tile([P, rows, NODES], F32, name="staged")
            outs = hop1_outs if hop == 1 else hop2_outs
            product_to_hbm(copy, codes, scales, s, j, staging[hop], outs[s], g, b, alone)

        for n in range(len(slices) + LAG):
            if n < len(slices):
                g, s, b, j = slices[n]
                cols = slice(j * P, (j + 1) * P)
                by_vector = n < VE and n % 2 == 1
                product(
                    1,
                    n,
                    nc.vector.tensor_copy if by_vector else nc.scalar.copy,
                    x_codes[g][:, b, cols],
                    x_scales[g][:, b, cols],
                    n < 2,
                )
                if not multiplied(n):
                    hop1_rows[n] = round_hop1(staging[1], j)
            if n >= LAG:
                codes, scales = hop1_quantised[(n - LAG) // QUAD]
                cols = slice((n - LAG) % QUAD * P, ((n - LAG) % QUAD + 1) * P)
                by_vector = (n - LAG) % VM == VR or n >= len(slices) and n % TA == 1
                product(
                    2,
                    n - LAG,
                    nc.vector.tensor_copy if by_vector else nc.scalar.copy,
                    codes[:, cols],
                    scales[:, cols],
                    n >= len(slices) + LAG - 4,
                )
            if n == S1:
                quantise_support(1, group_support(1, S1E))
            if n % 2 == 0:
                if FLIP_LAG <= n < len(slices) + FLIP_LAG:
                    k = n - FLIP_LAG
                    if k % QUAD == 0:
                        hop1_grouped[k // QUAD] = new_grouped()
                    grouped = hop1_grouped[k // QUAD]
                    if multiplied(k):
                        banks = [multiply_flipped(k + i) for i in range(2)]
                        for i in range(2):
                            group_multiplied(grouped, k % QUAD + i, banks[i])
                    else:
                        group_hop1(grouped, k % QUAD, flip_hop1((hop1_rows[k], hop1_rows[k + 1])))
                if x_banks and n >= X0 and (n % 4 == 2 or n <= XE):
                    g, i = x_banks.pop(0)
                    if i == 0:
                        new_group(g)
                    sort_x(nc.scalar.copy if n <= XE and i % 4 >= 4 - SX else nc.vector.tensor_copy, g, i, flip_x(g, i))
                    if i == GROUPS[g][2] // 2 - 1:
                        x_ready.extend((g, b) for b in range(PAIR))
            else:
                if FLIP_LAG <= n < len(slices) + FLIP_LAG:
                    k = n - FLIP_LAG
                    if k % QUAD == QUAD - 1:
                        hop1_quantised[k // QUAD] = quantise_hop1(hop1_grouped[k // QUAD])
                if x_ready:
                    quantise_x(*x_ready.pop(0))
